import numpy as np
import ml_dtypes


def mxq(x, axis, fmt="e4m3"):
    dtype, down = {"e4m3": (ml_dtypes.float8_e4m3fn, 7), "e5m2": (ml_dtypes.float8_e5m2, 14)}[fmt]
    v = np.moveaxis(np.asarray(x, np.float32).astype(ml_dtypes.bfloat16).astype(np.float64), axis, -1)
    blocks = v.reshape(v.shape[:-1] + (-1, 32))
    amax = np.abs(blocks).max(-1, keepdims=True)
    byte = np.maximum(np.where(amax > 0, np.frexp(amax)[1] - 1 + 127, 0) - down, 1)
    scale = np.exp2(byte - 127.0)
    codes = (blocks / scale).astype(np.float32).astype(dtype).astype(np.float64)
    return np.moveaxis((codes * scale).reshape(v.shape), -1, axis)


WIDE = False


def mx_kscale(k):
    if not WIDE:
        return np.ones(k)
    levels = np.array([10, -10, 5, -5, 0])
    a = np.random.permutation(np.resize(levels, k // 512 * 4)).reshape(k // 512, 4)
    idx = np.arange(k)
    return np.exp2(a[idx // 512, idx % 128 // 32])


BF16 = ml_dtypes.bfloat16


def bf(x):
    return np.asarray(x, np.float32).astype(BF16)


def f64(x):
    return np.asarray(x).astype(np.float64)


N, FIN, FD, F1, F2, F3, E = 1536, 2048, 1024, 512, 256, 128, 2


def elu(v):
    return np.where(v > 0.0, v, np.exp(np.minimum(v, 0.0)) - 1.0)


def setup_inputs():
    s = mx_kscale(FD)
    k = mx_kscale(N)
    t = np.where(np.arange(E) % 2 == 0, k.max(), k.min())
    return {
        "x": bf(elu(np.random.standard_normal((N, FD))) * s),
        "adjacency_matrix": bf(np.random.uniform(size=(E, N, N)) * 0.5 / np.sqrt(N) / t[:, None, None]),
        "W1": bf(np.random.standard_normal((E, FD, F1)) / np.sqrt(FD) / s[:, None] * t[:, None, None]),
        "b1": bf(np.random.standard_normal(F1) * 0.3),
        "Wr1": bf(np.random.standard_normal((FD, F1)) * 0.3 / np.sqrt(FD) / s[:, None]),
    }


def reference(x, adjacency_matrix, W1, b1, Wr1):
    xq = mxq(f64(x), 1, "e4m3")
    support = xq @ mxq(f64(W1), 1, "e4m3")
    agg = (mxq(f64(adjacency_matrix), 2, "e4m3") @ mxq(support, 1, "e4m3")).sum(0)
    return agg + f64(b1) + (xq @ mxq(f64(Wr1), 0, "e4m3"))

@@ -1,0 +1,296 @@
+from contextlib import ExitStack
+
+import concourse.mybir as mybir
+from concourse.masks import make_identity
+
+F32 = mybir.dt.float32
+BF16 = mybir.dt.bfloat16
+U32 = mybir.dt.uint32
+U8 = mybir.dt.uint8
+FP8X4 = mybir.dt.float8_e4m3fn_x4
+ADD = mybir.AluOpType.add
+P = 128
+FLOPS = 9663676416
+
+
+def tile_fgg_pa_kernel(tc, x, adjacency_matrix, W1, b1, Wr1, out):
+    nc = tc.nc
+    x_v = x.rearrange("(j p e) k -> j p (e k)", p=P, e=2)
+    adj_v = adjacency_matrix.rearrange("a (j p q) m -> a j p (q m)", p=P, q=2)
+    out_v = out.rearrange("(j p e) f -> j e p f", p=P, e=2)
+    with ExitStack() as ctx:
+        const = ctx.enter_context(tc.tile_pool(name="const", bufs=1))
+        rawp = ctx.enter_context(tc.tile_pool(name="rawp", bufs=12))
+        grpp = ctx.enter_context(tc.tile_pool(name="grpp", bufs=8))
+        keep = ctx.enter_context(tc.tile_pool(name="keep", bufs=1))
+        outp = ctx.enter_context(tc.tile_pool(name="outp", bufs=4))
+        psum = ctx.enter_context(tc.psum_pool(name="psum", bufs=1))
+        ctx.enter_context(tc.manual_schedule())
+        state = {"bank": 0}
+        V = nc.vector
+        S = nc.scalar
+
+        def new_bank(shape):
+            i = state["bank"]
+            state["bank"] = i + 1
+            return psum.tile(shape, F32, name="bank%d" % (i % 8), tag="bank%d" % (i % 8))
+
+        def new_raw():
+            return rawp.tile([P, 3072], BF16, name="raw", tag="raw")
+
+        def new_grp():
+            return grpp.tile([P, 2048], BF16, name="grp", tag="grp", align_bytes=64)
+
+        def copy_on(eng, dst, src):
+            if eng is S:
+                S.copy(out=dst, in_=src)
+            else:
+                V.tensor_copy(out=dst, in_=src)
+
+        def quantise(grp, nm):
+            c = keep.tile([P, 512], U32, name="c_" + nm, align_bytes=64)
+            s = keep.tile([P, 512], U8, name="s_" + nm, align_bytes=64)
+            V.quantize_mx(out=c[:].bitcast(FP8X4), scales=s[:], in_=grp[:])
+            return (c, s)
+
+        def mx(acc, lt, lcol, rt, rcol, n, start, stop):
+            nc.tensor.matmul_mx(
+                out=acc,
+                lhsT=lt[0][:, lcol : lcol + P].bitcast(FP8X4),
+                lhsT_scale=lt[1][:, lcol : lcol + P],
+                rhs=rt[0][:, rcol : rcol + n].bitcast(FP8X4),
+                rhs_scale=rt[1][:, rcol : rcol + n],
+                start=start,
+                stop=stop,
+            )
+
+        ident = const.tile([P, P], F32, name="ident")
+        make_identity(nc, ident[:])
+
+        xraw = {}
+        wraw = {}
+        araw = {}
+
+        def load_x(j):
+            t = new_raw()
+            nc.sync.dma_start(out=t[:, 0:2048], in_=x_v[j])
+            xraw[j] = t
+
+        def load_w(key, src, g):
+            t = new_raw()
+            nc.sync.dma_start(
+                out=t[:, 0:2048].rearrange("p (u r) -> p u r", u=2),
+                in_=src[512 * g : 512 * g + 512, :].rearrange("(u p q) c -> p u (q c)", u=2, p=P, q=2),
+            )
+            wraw[(key, g)] = t
+
+        def load_adj(i):
+            u, e = i // 2, i % 2
+            t = new_raw()
+            nc.sync.dma_start(out=t[:], in_=adj_v[e, u])
+            araw[(e, u)] = t
+
+        load_w(0, W1[0], 0)
+        load_x(0)
+        load_w(0, W1[0], 1)
+        load_x(1)
+        load_w(1, W1[1], 0)
+        load_w(1, W1[1], 1)
+        for j in range(2, 6):
+            load_x(j)
+        load_w(2, Wr1, 0)
+        load_w(2, Wr1, 1)
+        bias_bf = const.tile([P, 512], BF16, name="bias_bf")
+        nc.sync.dma_start(out=bias_bf[:], in_=b1.partition_broadcast(P))
+        bias_f = const.tile([P, 512], F32, name="bias_f")
+
+        wgrp = {}
+        wq = {}
+        xbank = {}
+        xgrp = {}
+        xq = {}
+        sbank = {}
+        sgrp = {}
+        sq = {}
+        abank = {}
+        agrp = {}
+        aq = {}
+
+        def rw(key, g):
+            grp = new_grp()
+            V.tensor_copy(
+                out=grp[:].rearrange("p (c i t) -> p c t i", i=4, t=4),
+                in_=wraw[(key, g)][:, 0:2048].rearrange("p (t c i) -> p c t i", t=4, i=4),
+            )
+            wgrp[(key, g)] = grp
+
+        def qw(key, g):
+            wq[(key, g)] = quantise(wgrp[(key, g)], "w%d%d" % (key, g))
+
+        def tx(tau):
+            w = xraw[tau // 2][:].bitcast(F32)
+            bank = new_bank([P, 2, 2, P])
+            for g in range(2):
+                for u in range(2):
+                    c0 = 512 * (tau % 2) + 256 * g + 128 * u
+                    nc.tensor.transpose(out=bank[:, g, u, :], in_=w[:, c0 : c0 + P], identity=ident[:])
+            xbank[tau] = bank
+
+        def words_out(eng, grp, half, bank):
+            copy_on(
+                eng,
+                grp[:].bitcast(F32)[:, 512 * half : 512 * half + 512].rearrange("p (o n u) -> p o n u", o=2, n=P, u=2),
+                bank[:].rearrange("p o u n -> p o n u"),
+            )
+
+        def cx(tau, eng):
+            if tau % 2 == 0:
+                xgrp[tau // 2] = new_grp()
+            words_out(eng, xgrp[tau // 2], tau % 2, xbank[tau])
+
+        def qx(i):
+            xq[i] = quantise(xgrp[i], "x%d" % i)
+
+        def sup(e, G, c):
+            bank = new_bank([P, 4, P])
+            for t in range(4):
+                tau = 4 * G + t
+                for g in range(2):
+                    mx(bank[:, t, :], xq[tau // 2], 256 * (tau % 2) + 128 * g, wq[(e, g)], 128 * c, P, g == 0, g == 1)
+            sbank[(e, G, c)] = bank
+
+        def cs(e, G, c, eng):
+            if c == 0:
+                sgrp[(e, G)] = new_grp()
+            copy_on(
+                eng,
+                sgrp[(e, G)][:, 512 * c : 512 * c + 512].rearrange("p (f t) -> p f t", t=4),
+                sbank[(e, G, c)][:].rearrange("p t f -> p f t"),
+            )
+
+        def qs(e, G):
+            sq[(e, G)] = quantise(sgrp[(e, G)], "s%d%d" % (e, G))
+
+        def ta(u, b):
+            bank = new_bank([P, 2, 2, P])
+            for o2 in range(2):
+                o = 2 * b + o2
+                w = araw[((o % 6) // 3, u)][:].bitcast(F32)
+                for u2 in range(2):
+                    c0 = 768 * (o // 6) + 256 * (o % 3) + 128 * u2
+                    nc.tensor.transpose(out=bank[:, o2, u2, :], in_=w[:, c0 : c0 + P], identity=ident[:])
+            abank[(u, b)] = bank
+
+        def ca(u, b, eng):
+            if b % 2 == 0:
+                agrp[(u, b // 2)] = new_grp()
+            words_out(eng, agrp[(u, b // 2)], b % 2, abank[(u, b)])
+
+        def qa(u, h):
+            aq[(u, h)] = quantise(agrp[(u, h)], "a%d%d" % (u, h))
+
+        def out_tile(u, q):
+            tau = 2 * u + q
+            acc = new_bank([P, 512])
+            for g in range(2):
+                mx(acc[:], xq[u], 256 * q + 128 * g, wq[(2, g)], 0, 512, g == 0, False)
+            for e in range(2):
+                for G in range(3):
+                    o = 6 * q + 3 * e + G
+                    mx(acc[:], aq[(u, o // 4)], 128 * (o % 4), sq[(e, G)], 0, 512, False, e == 1 and G == 2)
+            return acc
+
+        def ev(u, q, acc):
+            osb = outp.tile([P, 512], F32, name="osb", tag="osb")
+            V.tensor_tensor(out=osb[:], in0=acc[:], in1=bias_f[:], op=ADD)
+            nc.sync.dma_start(out=out_v[u, q], in_=osb[:])
+
+        def s_block(e, G, vshare):
+            for c in range(4):
+                sup(e, G, c)
+            for c in range(4):
+                cs(e, G, c, V if (vshare and c == 3) else S)
+
+        rw(0, 0)
+        qw(0, 0)
+        tx(0)
+        tx(1)
+        cx(0, S)
+        cx(1, S)
+        rw(0, 1)
+        qx(0)
+        qw(0, 1)
+        tx(2)
+        tx(3)
+        cx(2, S)
+        cx(3, S)
+        qx(1)
+        for i in range(4):
+            load_adj(i)
+        rw(1, 0)
+        rw(1, 1)
+        qw(1, 0)
+        qw(1, 1)
+        load_adj(4)
+        load_adj(5)
+        s_block(0, 0, False)
+        for tau in range(4, 8):
+            tx(tau)
+        for tau in range(4, 8):
+            cx(tau, S)
+        qs(0, 0)
+        qx(2)
+        qx(3)
+        load_adj(6)
+        load_adj(7)
+        s_block(1, 0, False)
+        for tau in range(8, 12):
+            tx(tau)
+        for tau in range(8, 12):
+            cx(tau, S)
+        rw(2, 0)
+        rw(2, 1)
+        qw(2, 0)
+        qw(2, 1)
+        V.tensor_copy(out=bias_f[:], in_=bias_bf[:])
+        for i in range(8, 12):
+            load_adj(i)
+        qs(1, 0)
+        qx(4)
+        qx(5)
+        s_block(0, 1, True)
+        s_block(1, 1, True)
+        qs(0, 1)
+
+        def t_block(u, vshare, first):
+            for b in range(6):
+                ta(u, b)
+            for f in first:
+                f()
+            if vshare:
+                for b in (0, 1, 3, 4):
+                    if b == 3:
+                        ca(u, 2, V)
+                    ca(u, b, S)
+                qa(u, 0)
+                ca(u, 5, V)
+                qa(u, 1)
+                qa(u, 2)
+            else:
+                for b in range(6):
+                    ca(u, b, S)
+                for h in range(3):
+                    qa(u, h)
+
+        t_block(0, True, [lambda: qs(1, 1)])
+        s_block(0, 2, True)
+        s_block(1, 2, True)
+        qs(0, 2)
+        t_block(1, True, [lambda: qs(1, 2)])
+        for u in range(6):
+            a0 = out_tile(u, 0)
+            a1 = out_tile(u, 1)
+            ev(u, 0, a0)
+            ev(u, 1, a1)
+            if u + 2 < 6:
+                t_block(u + 2, False, [])

@@ -47,10 +47,10 @@ def tile_fgg_pa_kernel(tc, x, adjacency_matrix, W1, b1, Wr1, out):
             else:
                 V.tensor_copy(out=dst, in_=src)
 
-        def quantise(grp, nm):
-            c = keep.tile([P, 512], U32, name="c_" + nm, align_bytes=64)
-            s = keep.tile([P, 512], U8, name="s_" + nm, align_bytes=64)
-            V.quantize_mx(out=c[:].bitcast(FP8X4), scales=s[:], in_=grp[:])
+        def quantise(grp, nm, lo=0, width=2048):
+            c = keep.tile([P, width // 4], U32, name="c_" + nm, align_bytes=64)
+            s = keep.tile([P, width // 4], U8, name="s_" + nm, align_bytes=64)
+            V.quantize_mx(out=c[:].bitcast(FP8X4), scales=s[:], in_=grp[:, lo : lo + width])
             return (c, s)
 
         def mx(acc, lt, lcol, rt, rcol, n, start, stop):
@@ -91,8 +91,8 @@ def tile_fgg_pa_kernel(tc, x, adjacency_matrix, W1, b1, Wr1, out):
             araw[(e, u)] = t
 
         load_w(0, W1[0], 0)
-        load_x(0)
         load_w(0, W1[0], 1)
+        load_x(0)
         load_x(1)
         load_w(1, W1[1], 0)
         load_w(1, W1[1], 1)
@@ -116,11 +116,12 @@ def tile_fgg_pa_kernel(tc, x, adjacency_matrix, W1, b1, Wr1, out):
         agrp = {}
         aq = {}
 
-        def rw(key, g):
+        def rw(key, g, eng=V):
             grp = new_grp()
-            V.tensor_copy(
-                out=grp[:].rearrange("p (c i t) -> p c t i", i=4, t=4),
-                in_=wraw[(key, g)][:, 0:2048].rearrange("p (t c i) -> p c t i", t=4, i=4),
+            copy_on(
+                eng,
+                grp[:].rearrange("p (c i t) -> p c t i", i=4, t=4),
+                wraw[(key, g)][:, 0:2048].rearrange("p (t c i) -> p c t i", t=4, i=4),
             )
             wgrp[(key, g)] = grp
 
@@ -149,15 +150,22 @@ def tile_fgg_pa_kernel(tc, x, adjacency_matrix, W1, b1, Wr1, out):
             words_out(eng, xgrp[tau // 2], tau % 2, xbank[tau])
 
         def qx(i):
-            xq[i] = quantise(xgrp[i], "x%d" % i)
+            pair = quantise(xgrp[i], "x%d" % i)
+            xq[2 * i] = (pair, 0)
+            xq[2 * i + 1] = (pair, 256)
+
+        def qx_one(tau):
+            xq[tau] = (quantise(xgrp[tau // 2], "xt%d" % tau, 1024 * (tau % 2), 1024), 0)
+
+        def sup_group(e, G, c, t):
+            tau = 4 * G + t
+            for g in range(2):
+                mx(sbank[(e, G, c)][:, t, :], xq[tau][0], xq[tau][1] + 128 * g, wq[(e, g)], 128 * c, P, g == 0, g == 1)
 
         def sup(e, G, c):
-            bank = new_bank([P, 4, P])
+            sbank[(e, G, c)] = new_bank([P, 4, P])
             for t in range(4):
-                tau = 4 * G + t
-                for g in range(2):
-                    mx(bank[:, t, :], xq[tau // 2], 256 * (tau % 2) + 128 * g, wq[(e, g)], 128 * c, P, g == 0, g == 1)
-            sbank[(e, G, c)] = bank
+                sup_group(e, G, c, t)
 
         def cs(e, G, c, eng):
             if c == 0:
@@ -193,38 +201,55 @@ def tile_fgg_pa_kernel(tc, x, adjacency_matrix, W1, b1, Wr1, out):
             tau = 2 * u + q
             acc = new_bank([P, 512])
             for g in range(2):
-                mx(acc[:], xq[u], 256 * q + 128 * g, wq[(2, g)], 0, 512, g == 0, False)
+                mx(acc[:], xq[tau][0], xq[tau][1] + 128 * g, wq[(2, g)], 0, 512, g == 0, False)
             for e in range(2):
                 for G in range(3):
                     o = 6 * q + 3 * e + G
                     mx(acc[:], aq[(u, o // 4)], 128 * (o % 4), sq[(e, G)], 0, 512, False, e == 1 and G == 2)
             return acc
 
+        def out_half(u, q, acc, half):
+            tau = 2 * u + q
+            dst = acc[:]
+            for g in range(2):
+                mx(dst, xq[tau][0], xq[tau][1] + 128 * g, wq[(2, g)], 256 * half, 256, g == 0, False)
+            for e in range(2):
+                for G in range(3):
+                    o = 6 * q + 3 * e + G
+                    mx(dst, aq[(u, o // 4)], 128 * (o % 4), sq[(e, G)], 256 * half, 256, False, e == 1 and G == 2)
+
+        def ev_half(u, q, acc, half):
+            cols = slice(256 * half, 256 * half + 256)
+            osb = outp.tile([P, 256], F32, name="osh", tag="osh")
+            V.tensor_tensor(out=osb[:], in0=acc[:], in1=bias_f[:, cols], op=ADD)
+            nc.sync.dma_start(out=out_v[u, q][:, cols], in_=osb[:])
+
         def ev(u, q, acc):
             osb = outp.tile([P, 512], F32, name="osb", tag="osb")
             V.tensor_tensor(out=osb[:], in0=acc[:], in1=bias_f[:], op=ADD)
             nc.sync.dma_start(out=out_v[u, q], in_=osb[:])
 
-        def s_block(e, G, vshare):
+        def s_block(e, G, vshare, before=None):
             for c in range(4):
                 sup(e, G, c)
+            if before is not None:
+                qs(before[0], before[1])
             for c in range(4):
                 cs(e, G, c, V if (vshare and c == 3) else S)
 
         rw(0, 0)
-        qw(0, 0)
-        tx(0)
-        tx(1)
-        cx(0, S)
-        cx(1, S)
         rw(0, 1)
-        qx(0)
+        qw(0, 0)
         qw(0, 1)
-        tx(2)
-        tx(3)
-        cx(2, S)
-        cx(3, S)
-        qx(1)
+        for tau in range(4):
+            tx(tau)
+        for c in range(4):
+            sbank[(0, 0, c)] = new_bank([P, 4, P])
+        for tau in range(4):
+            cx(tau, S)
+            qx_one(tau)
+            for c in range(4):
+                sup_group(0, 0, c, tau)
         for i in range(4):
             load_adj(i)
         rw(1, 0)
@@ -233,7 +258,8 @@ def tile_fgg_pa_kernel(tc, x, adjacency_matrix, W1, b1, Wr1, out):
         qw(1, 1)
         load_adj(4)
         load_adj(5)
-        s_block(0, 0, False)
+        for c in range(4):
+            cs(0, 0, c, S)
         for tau in range(4, 8):
             tx(tau)
         for tau in range(4, 8):
@@ -259,38 +285,39 @@ def tile_fgg_pa_kernel(tc, x, adjacency_matrix, W1, b1, Wr1, out):
         qx(4)
         qx(5)
         s_block(0, 1, True)
-        s_block(1, 1, True)
-        qs(0, 1)
+        s_block(1, 1, True, (0, 1))
 
-        def t_block(u, vshare, first):
+        def t_unit(u, vbanks):
             for b in range(6):
                 ta(u, b)
-            for f in first:
-                f()
-            if vshare:
-                for b in (0, 1, 3, 4):
-                    if b == 3:
-                        ca(u, 2, V)
-                    ca(u, b, S)
-                qa(u, 0)
-                ca(u, 5, V)
-                qa(u, 1)
-                qa(u, 2)
-            else:
-                for b in range(6):
-                    ca(u, b, S)
-                for h in range(3):
-                    qa(u, h)
+                ca(u, b, V if b in vbanks else S)
+                if b == 4:
+                    qa(u, 0)
+            qa(u, 1)
+            qa(u, 2)
 
-        t_block(0, True, [lambda: qs(1, 1)])
+        VBA = (2, 5)
+        VBB = (5,)
+        qs(1, 1)
+        t_unit(0, VBA)
         s_block(0, 2, True)
-        s_block(1, 2, True)
-        qs(0, 2)
-        t_block(1, True, [lambda: qs(1, 2)])
-        for u in range(6):
-            a0 = out_tile(u, 0)
-            a1 = out_tile(u, 1)
-            ev(u, 0, a0)
-            ev(u, 1, a1)
-            if u + 2 < 6:
-                t_block(u + 2, False, [])
+        s_block(1, 2, True, (0, 2))
+        qs(1, 2)
+        t_unit(1, VBA)
+        for q in range(2):
+            ev(0, q, out_tile(0, q))
+        t_unit(2, VBB)
+        t_unit(3, VBB)
+        for u in (1, 2):
+            for q in range(2):
+                ev(u, q, out_tile(u, q))
+        t_unit(4, VBB)
+        t_unit(5, VBB)
+        for u in (3, 4):
+            for q in range(2):
+                ev(u, q, out_tile(u, q))
+        ev(5, 0, out_tile(5, 0))
+        for half in range(2):
+            last = new_bank([P, 256])
+            out_half(5, 1, last, half)
+            ev_half(5, 1, last, half)

@@ -17,12 +17,15 @@ def tile_fgg_pa_kernel(tc, x, adjacency_matrix, W1, b1, Wr1, out):
     nc = tc.nc
     x_v = x.rearrange("(j p e) k -> j p (e k)", p=P, e=2)
     adj_v = adjacency_matrix.rearrange("a (j p q) m -> a j p (q m)", p=P, q=2)
+    adj_q = adjacency_matrix.rearrange("a (j p q) m -> a j p q m", p=P, q=2)
+    adj_s = adjacency_matrix.rearrange("a (jb n q) m -> a q n jb m", n=16, q=2)
     out_v = out.rearrange("(j p e) f -> j e p f", p=P, e=2)
     with ExitStack() as ctx:
         const = ctx.enter_context(tc.tile_pool(name="const", bufs=1))
         rawp = ctx.enter_context(tc.tile_pool(name="rawp", bufs=12))
         grpp = ctx.enter_context(tc.tile_pool(name="grpp", bufs=8))
         keep = ctx.enter_context(tc.tile_pool(name="keep", bufs=1))
+        zpool = ctx.enter_context(tc.tile_pool(name="zpool", bufs=1))
         outp = ctx.enter_context(tc.tile_pool(name="outp", bufs=4))
         psum = ctx.enter_context(tc.psum_pool(name="psum", bufs=1))
         ctx.enter_context(tc.manual_schedule())
@@ -67,6 +70,8 @@ def tile_fgg_pa_kernel(tc, x, adjacency_matrix, W1, b1, Wr1, out):
         ident = const.tile([P, P], F32, name="ident")
         make_identity(nc, ident[:])
 
+        VU = (2, 3, 4, 5)
+        zt = {}
         xraw = {}
         wraw = {}
         araw = {}
@@ -87,8 +92,25 @@ def tile_fgg_pa_kernel(tc, x, adjacency_matrix, W1, b1, Wr1, out):
         def load_adj(i):
             u, e = i // 2, i % 2
             t = new_raw()
-            nc.sync.dma_start(out=t[:], in_=adj_v[e, u])
+            if u in VU:
+                nc.sync.dma_start(out=t[:, 0:2048].rearrange("p (q m) -> p q m", q=2), in_=adj_q[e, u][:, :, 0:1024])
+            else:
+                nc.sync.dma_start(out=t[:], in_=adj_v[e, u])
             araw[(e, u)] = t
+
+        def load_slow(u0):
+            for q in range(2):
+                for e in range(2):
+                    z = zpool.tile([P, 1024], BF16, name="z%d%d%d" % (u0, q, e), align_bytes=64)
+                    for a in range(4):
+                        for u2 in range(2):
+                            c0 = 1024 + 256 * u2 + 64 * a
+                            nc.sync.dma_start(
+                                out=z[32 * a + u2 : 32 * a + 32 : 2, :].rearrange("p (jb m) -> p jb m", m=64),
+                                in_=adj_s[e, q, :, 8 * u0 : 8 * u0 + 16, c0 : c0 + 64],
+                            )
+                    zt[(u0, q, e)] = z
+                    zt[(u0 + 1, q, e)] = z
 
         load_w(0, W1[0], 0)
         load_w(0, W1[0], 1)
@@ -183,11 +205,34 @@ def tile_fgg_pa_kernel(tc, x, adjacency_matrix, W1, b1, Wr1, out):
             bank = new_bank([P, 2, 2, P])
             for o2 in range(2):
                 o = 2 * b + o2
-                w = araw[((o % 6) // 3, u)][:].bitcast(F32)
+                if u in VU:
+                    q, e, G, row = o // 4, (o % 4) // 2, o % 2, 512
+                else:
+                    q, e, G, row = o // 6, (o % 6) // 3, o % 3, 768
+                w = araw[(e, u)][:].bitcast(F32)
                 for u2 in range(2):
-                    c0 = 768 * (o // 6) + 256 * (o % 3) + 128 * u2
+                    c0 = row * q + 256 * G + 128 * u2
                     nc.tensor.transpose(out=bank[:, o2, u2, :], in_=w[:, c0 : c0 + P], identity=ident[:])
             abank[(u, b)] = bank
+
+        def vt(u):
+            grp = new_grp()
+            for q in range(2):
+                for e in range(2):
+                    V.transpose(
+                        out=grp[:].bitcast(F32)[:, 256 * (2 * q + e) : 256 * (2 * q + e) + 256],
+                        in_=zt[(u, q, e)][:].bitcast(F32)[:, 256 * (u % 2) : 256 * (u % 2) + 256],
+                    )
+            agrp[(u, 2)] = grp
+
+        def operand(u, q, e, G):
+            if u not in VU:
+                o = 6 * q + 3 * e + G
+            elif G < 2:
+                o = 4 * q + 2 * e + G
+            else:
+                o = 8 + 2 * q + e
+            return (aq[(u, o // 4)], 128 * (o % 4))
 
         def ca(u, b, eng):
             if b % 2 == 0:
@@ -204,8 +249,8 @@ def tile_fgg_pa_kernel(tc, x, adjacency_matrix, W1, b1, Wr1, out):
                 mx(acc[:], xq[tau][0], xq[tau][1] + 128 * g, wq[(2, g)], 0, 512, g == 0, False)
             for e in range(2):
                 for G in range(3):
-                    o = 6 * q + 3 * e + G
-                    mx(acc[:], aq[(u, o // 4)], 128 * (o % 4), sq[(e, G)], 0, 512, False, e == 1 and G == 2)
+                    lt = operand(u, q, e, G)
+                    mx(acc[:], lt[0], lt[1], sq[(e, G)], 0, 512, False, e == 1 and G == 2)
             return acc
 
         def out_half(u, q, acc, half):
@@ -215,8 +260,8 @@ def tile_fgg_pa_kernel(tc, x, adjacency_matrix, W1, b1, Wr1, out):
                 mx(dst, xq[tau][0], xq[tau][1] + 128 * g, wq[(2, g)], 256 * half, 256, g == 0, False)
             for e in range(2):
                 for G in range(3):
-                    o = 6 * q + 3 * e + G
-                    mx(dst, aq[(u, o // 4)], 128 * (o % 4), sq[(e, G)], 256 * half, 256, False, e == 1 and G == 2)
+                    lt = operand(u, q, e, G)
+                    mx(dst, lt[0], lt[1], sq[(e, G)], 256 * half, 256, False, e == 1 and G == 2)
 
         def ev_half(u, q, acc, half):
             cols = slice(256 * half, 256 * half + 256)
@@ -279,8 +324,10 @@ def tile_fgg_pa_kernel(tc, x, adjacency_matrix, W1, b1, Wr1, out):
         qw(2, 0)
         qw(2, 1)
         V.tensor_copy(out=bias_f[:], in_=bias_bf[:])
+        load_slow(2)
         for i in range(8, 12):
             load_adj(i)
+        load_slow(4)
         qs(1, 0)
         qx(4)
         qx(5)
@@ -296,8 +343,12 @@ def tile_fgg_pa_kernel(tc, x, adjacency_matrix, W1, b1, Wr1, out):
             qa(u, 1)
             qa(u, 2)
 
+        def t_short(u):
+            for b in range(4):
+                ta(u, b)
+                ca(u, b, S)
+
         VBA = (2, 5)
-        VBB = (5,)
         qs(1, 1)
         t_unit(0, VBA)
         s_block(0, 2, True)
@@ -306,16 +357,34 @@ def tile_fgg_pa_kernel(tc, x, adjacency_matrix, W1, b1, Wr1, out):
         t_unit(1, VBA)
         for q in range(2):
             ev(0, q, out_tile(0, q))
-        t_unit(2, VBB)
-        t_unit(3, VBB)
-        for u in (1, 2):
-            for q in range(2):
-                ev(u, q, out_tile(u, q))
-        t_unit(4, VBB)
-        t_unit(5, VBB)
-        for u in (3, 4):
-            for q in range(2):
-                ev(u, q, out_tile(u, q))
+        t_short(2)
+        t_short(3)
+        qa(2, 0)
+        qa(2, 1)
+        vt(2)
+        qa(3, 0)
+        qa(2, 2)
+        qa(3, 1)
+        for q in range(2):
+            ev(1, q, out_tile(1, q))
+        vt(3)
+        ev(2, 0, out_tile(2, 0))
+        qa(3, 2)
+        ev(2, 1, out_tile(2, 1))
+        t_short(4)
+        t_short(5)
+        qa(4, 0)
+        qa(4, 1)
+        vt(4)
+        qa(5, 0)
+        qa(4, 2)
+        qa(5, 1)
+        for q in range(2):
+            ev(3, q, out_tile(3, q))
+        vt(5)
+        ev(4, 0, out_tile(4, 0))
+        qa(5, 2)
+        ev(4, 1, out_tile(4, 1))
         ev(5, 0, out_tile(5, 0))
         for half in range(2):
             last = new_bank([P, 256])

@@ -26,10 +26,10 @@ def tile_fgg_pa_kernel(tc, x, adjacency_matrix, W1, b1, Wr1, out):
         grpp = ctx.enter_context(tc.tile_pool(name="grpp", bufs=8))
         keep = ctx.enter_context(tc.tile_pool(name="keep", bufs=1))
         zpool = ctx.enter_context(tc.tile_pool(name="zpool", bufs=1))
-        outp = ctx.enter_context(tc.tile_pool(name="outp", bufs=4))
+        outp = ctx.enter_context(tc.tile_pool(name="outp", bufs=8))
         psum = ctx.enter_context(tc.psum_pool(name="psum", bufs=1))
         ctx.enter_context(tc.manual_schedule())
-        state = {"bank": 0}
+        state = {"bank": 0, "next": 0}
         V = nc.vector
         S = nc.scalar
 
@@ -70,7 +70,7 @@ def tile_fgg_pa_kernel(tc, x, adjacency_matrix, W1, b1, Wr1, out):
         ident = const.tile([P, P], F32, name="ident")
         make_identity(nc, ident[:])
 
-        VU = (2, 3, 4, 5)
+        VU = (4, 5)
         zt = {}
         xraw = {}
         wraw = {}
@@ -98,19 +98,33 @@ def tile_fgg_pa_kernel(tc, x, adjacency_matrix, W1, b1, Wr1, out):
                 nc.sync.dma_start(out=t[:], in_=adj_v[e, u])
             araw[(e, u)] = t
 
-        def load_slow(u0):
+        def slow_tiles(u0):
             for q in range(2):
                 for e in range(2):
                     z = zpool.tile([P, 1024], BF16, name="z%d%d%d" % (u0, q, e), align_bytes=64)
-                    for a in range(4):
-                        for u2 in range(2):
-                            c0 = 1024 + 256 * u2 + 64 * a
-                            nc.sync.dma_start(
-                                out=z[32 * a + u2 : 32 * a + 32 : 2, :].rearrange("p (jb m) -> p jb m", m=64),
-                                in_=adj_s[e, q, :, 8 * u0 : 8 * u0 + 16, c0 : c0 + 64],
-                            )
                     zt[(u0, q, e)] = z
                     zt[(u0 + 1, q, e)] = z
+
+        def load_slow(u0, k):
+            q, e, a, u2 = k // 16, (k // 8) % 2, (k // 2) % 4, k % 2
+            c0 = 1024 + 256 * u2 + 64 * a
+            nc.sync.dma_start(
+                out=zt[(u0, q, e)][32 * a + u2 : 32 * a + 32 : 2, :].rearrange("p (jb m) -> p jb m", m=64),
+                in_=adj_s[e, q, :, 8 * u0 : 8 * u0 + 16, c0 : c0 + 64],
+            )
+
+        queue = []
+
+        def pump(allowed):
+            while state["next"] < len(queue):
+                item = queue[state["next"]]
+                if item[0] == "adj" and item[1] > allowed:
+                    return
+                state["next"] = state["next"] + 1
+                if item[0] == "adj":
+                    load_adj(item[1])
+                else:
+                    load_slow(item[1], item[2])
 
         load_w(0, W1[0], 0)
         load_w(0, W1[0], 1)
@@ -125,6 +139,11 @@ def tile_fgg_pa_kernel(tc, x, adjacency_matrix, W1, b1, Wr1, out):
         bias_bf = const.tile([P, 512], BF16, name="bias_bf")
         nc.sync.dma_start(out=bias_bf[:], in_=b1.partition_broadcast(P))
         bias_f = const.tile([P, 512], F32, name="bias_f")
+        slow_tiles(4)
+        queue.extend([("adj", i) for i in range(6)])
+        for i in range(6, 12):
+            queue.append(("adj", i))
+            queue.extend([("slow", 4, k) for k in range(32) if k * 6 // 32 == i - 6])
 
         wgrp = {}
         wq = {}
@@ -265,7 +284,7 @@ def tile_fgg_pa_kernel(tc, x, adjacency_matrix, W1, b1, Wr1, out):
 
         def ev_half(u, q, acc, half):
             cols = slice(256 * half, 256 * half + 256)
-            osb = outp.tile([P, 256], F32, name="osh", tag="osh")
+            osb = outp.tile([P, 256], F32, name="osh", tag="osh", bufs=2)
             V.tensor_tensor(out=osb[:], in0=acc[:], in1=bias_f[:, cols], op=ADD)
             nc.sync.dma_start(out=out_v[u, q][:, cols], in_=osb[:])
 
@@ -295,14 +314,12 @@ def tile_fgg_pa_kernel(tc, x, adjacency_matrix, W1, b1, Wr1, out):
             qx_one(tau)
             for c in range(4):
                 sup_group(0, 0, c, tau)
-        for i in range(4):
-            load_adj(i)
+        pump(3)
         rw(1, 0)
         rw(1, 1)
         qw(1, 0)
         qw(1, 1)
-        load_adj(4)
-        load_adj(5)
+        pump(5)
         for c in range(4):
             cs(0, 0, c, S)
         for tau in range(4, 8):
@@ -312,8 +329,7 @@ def tile_fgg_pa_kernel(tc, x, adjacency_matrix, W1, b1, Wr1, out):
         qs(0, 0)
         qx(2)
         qx(3)
-        load_adj(6)
-        load_adj(7)
+        pump(7)
         s_block(1, 0, False)
         for tau in range(8, 12):
             tx(tau)
@@ -324,10 +340,7 @@ def tile_fgg_pa_kernel(tc, x, adjacency_matrix, W1, b1, Wr1, out):
         qw(2, 0)
         qw(2, 1)
         V.tensor_copy(out=bias_f[:], in_=bias_bf[:])
-        load_slow(2)
-        for i in range(8, 12):
-            load_adj(i)
-        load_slow(4)
+        pump(11)
         qs(1, 0)
         qx(4)
         qx(5)
@@ -357,20 +370,11 @@ def tile_fgg_pa_kernel(tc, x, adjacency_matrix, W1, b1, Wr1, out):
         t_unit(1, VBA)
         for q in range(2):
             ev(0, q, out_tile(0, q))
-        t_short(2)
-        t_short(3)
-        qa(2, 0)
-        qa(2, 1)
-        vt(2)
-        qa(3, 0)
-        qa(2, 2)
-        qa(3, 1)
-        for q in range(2):
-            ev(1, q, out_tile(1, q))
-        vt(3)
-        ev(2, 0, out_tile(2, 0))
-        qa(3, 2)
-        ev(2, 1, out_tile(2, 1))
+        t_unit(2, (5,))
+        t_unit(3, (5,))
+        for u in (1, 2):
+            for q in range(2):
+                ev(u, q, out_tile(u, q))
         t_short(4)
         t_short(5)
         qa(4, 0)

@@ -69,6 +69,13 @@ def tile_fgg_pa_kernel(tc, x, adjacency_matrix, W1, b1, Wr1, out):
 
         ident = const.tile([P, P], F32, name="ident")
         make_identity(nc, ident[:])
+        zeros = const.tile([P, 512], BF16, name="zeros")
+        V.memset(zeros[:], 0.0)
+
+        def warm(count):
+            bank = psum.tile([P, 512], F32, name="bank7", tag="bank7")
+            for i in range(count):
+                nc.tensor.matmul(out=bank[:], lhsT=zeros[:, 0:P], rhs=zeros[:], start=True, stop=True)
 
         VU = (4, 5)
         zt = {}
@@ -301,6 +308,7 @@ def tile_fgg_pa_kernel(tc, x, adjacency_matrix, W1, b1, Wr1, out):
             for c in range(4):
                 cs(e, G, c, V if (vshare and c == 3) else S)
 
+        warm(10)
         rw(0, 0)
         rw(0, 1)
         qw(0, 0)

@@ -143,8 +143,11 @@ def tile_fgg_pa_kernel(tc, x, adjacency_matrix, W1, b1, Wr1, out):
             load_x(j)
         load_w(2, Wr1, 0)
         load_w(2, Wr1, 1)
-        bias_bf = const.tile([P, 512], BF16, name="bias_bf")
-        nc.sync.dma_start(out=bias_bf[:], in_=b1.partition_broadcast(P))
+        bias_row = const.tile([P, 512], BF16, name="bias_row")
+        V.memset(bias_row[:], 0.0)
+        nc.sync.dma_start(out=bias_row[0:1, :], in_=b1.unsqueeze(0))
+        ones = const.tile([P, P], BF16, name="ones")
+        V.memset(ones[:], 1.0)
         bias_f = const.tile([P, 512], F32, name="bias_f")
         slow_tiles(4)
         queue.extend([("adj", i) for i in range(6)])
@@ -164,13 +167,16 @@ def tile_fgg_pa_kernel(tc, x, adjacency_matrix, W1, b1, Wr1, out):
         agrp = {}
         aq = {}
 
-        def rw(key, g, eng=V):
+        def rw(key, g, scalar_cols=0):
             grp = new_grp()
-            copy_on(
-                eng,
-                grp[:].rearrange("p (c i t) -> p c t i", i=4, t=4),
-                wraw[(key, g)][:, 0:2048].rearrange("p (t c i) -> p c t i", t=4, i=4),
-            )
+            cut = (512 - scalar_cols) // 4
+            for eng, lo, hi in ((V, 0, cut), (S, cut, 128)):
+                if lo < hi:
+                    copy_on(
+                        eng,
+                        grp[:].rearrange("p (c i t) -> p c t i", i=4, t=4)[:, lo:hi],
+                        wraw[(key, g)][:, 0:2048].rearrange("p (t c i) -> p c t i", t=4, i=4)[:, lo:hi],
+                    )
             wgrp[(key, g)] = grp
 
         def qw(key, g):
@@ -347,7 +353,9 @@ def tile_fgg_pa_kernel(tc, x, adjacency_matrix, W1, b1, Wr1, out):
         rw(2, 1)
         qw(2, 0)
         qw(2, 1)
-        V.tensor_copy(out=bias_f[:], in_=bias_bf[:])
+        bias_bank = new_bank([P, 512])
+        nc.tensor.matmul(out=bias_bank[:], lhsT=ones[:], rhs=bias_row[:], start=True, stop=True)
+        S.copy(out=bias_f[:], in_=bias_bank[:])
         pump(11)
         qs(1, 0)
         qx(4)

@@ -6,6 +6,7 @@ from concourse.masks import make_identity
 F32 = mybir.dt.float32
 BF16 = mybir.dt.bfloat16
 U32 = mybir.dt.uint32
+I32 = mybir.dt.int32
 U8 = mybir.dt.uint8
 FP8X4 = mybir.dt.float8_e4m3fn_x4
 ADD = mybir.AluOpType.add
@@ -16,17 +17,17 @@ FLOPS = 9663676416
 def tile_fgg_pa_kernel(tc, x, adjacency_matrix, W1, b1, Wr1, out):
     nc = tc.nc
     x_v = x.rearrange("(j p e) k -> j p (e k)", p=P, e=2)
-    adj_v = adjacency_matrix.rearrange("a (j p q) m -> a j p (q m)", p=P, q=2)
     adj_q = adjacency_matrix.rearrange("a (j p q) m -> a j p q m", p=P, q=2)
-    adj_s = adjacency_matrix.rearrange("a (jb n q) m -> a q n jb m", n=16, q=2)
+    adj_r = adjacency_matrix.rearrange("a (j b r q) m -> a j q r b m", b=4, r=32, q=2)
     out_v = out.rearrange("(j p e) f -> j e p f", p=P, e=2)
     with ExitStack() as ctx:
         const = ctx.enter_context(tc.tile_pool(name="const", bufs=1))
-        rawp = ctx.enter_context(tc.tile_pool(name="rawp", bufs=12))
+        rawp = ctx.enter_context(tc.tile_pool(name="rawp", bufs=16))
         grpp = ctx.enter_context(tc.tile_pool(name="grpp", bufs=8))
+        turn = ctx.enter_context(tc.tile_pool(name="turn", bufs=3))
         keep = ctx.enter_context(tc.tile_pool(name="keep", bufs=1))
-        zpool = ctx.enter_context(tc.tile_pool(name="zpool", bufs=1))
-        outp = ctx.enter_context(tc.tile_pool(name="outp", bufs=8))
+        adjp = ctx.enter_context(tc.tile_pool(name="adjp", bufs=4))
+        outp = ctx.enter_context(tc.tile_pool(name="outp", bufs=6))
         psum = ctx.enter_context(tc.psum_pool(name="psum", bufs=1))
         ctx.enter_context(tc.manual_schedule())
         state = {"bank": 0, "next": 0}
@@ -39,7 +40,7 @@ def tile_fgg_pa_kernel(tc, x, adjacency_matrix, W1, b1, Wr1, out):
             return psum.tile(shape, F32, name="bank%d" % (i % 8), tag="bank%d" % (i % 8))
 
         def new_raw():
-            return rawp.tile([P, 3072], BF16, name="raw", tag="raw")
+            return rawp.tile([P, 2048], BF16, name="raw", tag="raw", align_bytes=64)
 
         def new_grp():
             return grpp.tile([P, 2048], BF16, name="grp", tag="grp", align_bytes=64)
@@ -50,9 +51,9 @@ def tile_fgg_pa_kernel(tc, x, adjacency_matrix, W1, b1, Wr1, out):
             else:
                 V.tensor_copy(out=dst, in_=src)
 
-        def quantise(grp, nm, lo=0, width=2048):
-            c = keep.tile([P, width // 4], U32, name="c_" + nm, align_bytes=64)
-            s = keep.tile([P, width // 4], U8, name="s_" + nm, align_bytes=64)
+        def quantise(grp, nm, lo=0, width=2048, pool=keep, filled=False):
+            c = pool.tile([P, width // 4], U32, name="c_" + nm, align_bytes=64)
+            s = pool.tile([P, width // 4], U8, name="s_" + nm, align_bytes=64)
             V.quantize_mx(out=c[:].bitcast(FP8X4), scales=s[:], in_=grp[:, lo : lo + width])
             return (c, s)
 
@@ -67,105 +68,103 @@ def tile_fgg_pa_kernel(tc, x, adjacency_matrix, W1, b1, Wr1, out):
                 stop=stop,
             )
 
-        ident = const.tile([P, P], F32, name="ident")
-        make_identity(nc, ident[:])
         zeros = const.tile([P, 512], BF16, name="zeros")
         V.memset(zeros[:], 0.0)
+        ident = const.tile([P, P], F32, name="ident")
+        make_identity(nc, ident[:])
+        bias_bf = const.tile([P, 512], BF16, name="bias_bf")
+        bias_f = const.tile([P, 512], F32, name="bias_f")
+        xpair = {}
+        for j in range(6):
+            c = keep.tile([P, 512], U32, name="c_x%d" % j, align_bytes=64)
+            s = keep.tile([P, 512], U8, name="s_x%d" % j, align_bytes=64)
+            if j < 4:
+                nc.gpsimd.memset(s[:].bitcast(U32), 0)
+            xpair[j] = (c, s)
+        xv_c = keep.tile([P, 16, P], U32, name="xv_c", align_bytes=64)
+        xv_s = keep.tile([P, 16, P], U8, name="xv_s", align_bytes=64)
 
-        def warm(count):
-            bank = psum.tile([P, 512], F32, name="bank7", tag="bank7")
-            for i in range(count):
-                nc.tensor.matmul(out=bank[:], lhsT=zeros[:, 0:P], rhs=zeros[:], start=True, stop=True)
-
-        VU = (4, 5)
-        zt = {}
         xraw = {}
         wraw = {}
         araw = {}
 
-        def load_x(j):
-            t = new_raw()
-            nc.sync.dma_start(out=t[:, 0:2048], in_=x_v[j])
-            xraw[j] = t
+        def load_x(j, halves=(0, 1)):
+            if 0 in halves:
+                xraw[j] = new_raw()
+            cols = slice(1024 * halves[0], 1024 * halves[-1] + 1024)
+            nc.sync.dma_start(out=xraw[j][:, cols], in_=x_v[j][:, cols])
 
         def load_w(key, src, g):
             t = new_raw()
             nc.sync.dma_start(
-                out=t[:, 0:2048].rearrange("p (u r) -> p u r", u=2),
+                out=t[:].rearrange("p (u r) -> p u r", u=2),
                 in_=src[512 * g : 512 * g + 512, :].rearrange("(u p q) c -> p u (q c)", u=2, p=P, q=2),
             )
             wraw[(key, g)] = t
 
-        def load_adj(i):
-            u, e = i // 2, i % 2
+        def load_blocks(u):
             t = new_raw()
-            if u in VU:
-                nc.sync.dma_start(out=t[:, 0:2048].rearrange("p (q m) -> p q m", q=2), in_=adj_q[e, u][:, :, 0:1024])
-            else:
-                nc.sync.dma_start(out=t[:], in_=adj_v[e, u])
-            araw[(e, u)] = t
-
-        def slow_tiles(u0):
+            z = t[:].rearrange("p (q b m) -> p q b m", q=2, b=4)
             for q in range(2):
-                for e in range(2):
-                    z = zpool.tile([P, 1024], BF16, name="z%d%d%d" % (u0, q, e), align_bytes=64)
-                    zt[(u0, q, e)] = z
-                    zt[(u0 + 1, q, e)] = z
+                for a in range(4):
+                    nc.sync.dma_start(
+                        out=z[32 * a : 32 * a + 32, q],
+                        in_=adj_r[1, u, q][:, :, 256 * a : 256 * a + 256],
+                    )
+            araw[("z", u)] = t
 
-        def load_slow(u0, k):
-            q, e, a, u2 = k // 16, (k // 8) % 2, (k // 2) % 4, k % 2
-            c0 = 1024 + 256 * u2 + 64 * a
-            nc.sync.dma_start(
-                out=zt[(u0, q, e)][32 * a + u2 : 32 * a + 32 : 2, :].rearrange("p (jb m) -> p jb m", m=64),
-                in_=adj_s[e, q, :, 8 * u0 : 8 * u0 + 16, c0 : c0 + 64],
-            )
+        def load_rows(u):
+            t = new_raw()
+            nc.sync.dma_start(out=t[:].rearrange("p (q m) -> p q m", q=2), in_=adj_q[0, u][:, :, 0:1024])
+            araw[("r", u)] = t
+
+        def load_last(u):
+            t = new_raw()
+            for e in range(2):
+                nc.sync.dma_start(
+                    out=t[:, 1024 * e : 1024 * e + 1024].rearrange("p (q m) -> p q m", q=2),
+                    in_=adj_q[e, u][:, :, 1024:1536],
+                )
+            araw[("g", u)] = t
 
         queue = []
+        for u in range(6):
+            queue.extend([(load_rows, u), (load_last, u), (load_blocks, u)])
 
-        def pump(allowed):
-            while state["next"] < len(queue):
-                item = queue[state["next"]]
-                if item[0] == "adj" and item[1] > allowed:
-                    return
+        def pump(count):
+            while state["next"] < min(count, len(queue)):
+                fn, u = queue[state["next"]]
+                fn(u)
                 state["next"] = state["next"] + 1
-                if item[0] == "adj":
-                    load_adj(item[1])
-                else:
-                    load_slow(item[1], item[2])
 
         load_w(0, W1[0], 0)
         load_w(0, W1[0], 1)
-        load_x(0)
-        load_x(1)
+        for j in range(4):
+            load_x(j)
         load_w(1, W1[1], 0)
         load_w(1, W1[1], 1)
-        for j in range(2, 6):
-            load_x(j)
+        load_x(4)
+        load_x(5)
         load_w(2, Wr1, 0)
         load_w(2, Wr1, 1)
-        bias_row = const.tile([P, 512], BF16, name="bias_row")
-        V.memset(bias_row[:], 0.0)
-        nc.sync.dma_start(out=bias_row[0:1, :], in_=b1.unsqueeze(0))
-        ones = const.tile([P, P], BF16, name="ones")
-        V.memset(ones[:], 1.0)
-        bias_f = const.tile([P, 512], F32, name="bias_f")
-        slow_tiles(4)
-        queue.extend([("adj", i) for i in range(6)])
-        for i in range(6, 12):
-            queue.append(("adj", i))
-            queue.extend([("slow", 4, k) for k in range(32) if k * 6 // 32 == i - 6])
+        nc.sync.dma_start(out=bias_bf[:], in_=b1.partition_broadcast(P))
+        pump(16 - 12)
 
         wgrp = {}
         wq = {}
         xbank = {}
         xgrp = {}
-        xq = {}
         sbank = {}
         sgrp = {}
         sq = {}
         abank = {}
         agrp = {}
         aq = {}
+
+        def warm(count):
+            bank = psum.tile([P, 512], F32, name="bank7", tag="bank7")
+            for i in range(count):
+                nc.tensor.matmul(out=bank[:], lhsT=zeros[:, 0:P], rhs=zeros[:], start=True, stop=True)
 
         def rw(key, g, scalar_cols=0):
             grp = new_grp()
@@ -175,7 +174,7 @@ def tile_fgg_pa_kernel(tc, x, adjacency_matrix, W1, b1, Wr1, out):
                     copy_on(
                         eng,
                         grp[:].rearrange("p (c i t) -> p c t i", i=4, t=4)[:, lo:hi],
-                        wraw[(key, g)][:, 0:2048].rearrange("p (t c i) -> p c t i", t=4, i=4)[:, lo:hi],
+                        wraw[(key, g)][:].rearrange("p (t c i) -> p c t i", t=4, i=4)[:, lo:hi],
                     )
             wgrp[(key, g)] = grp
 
@@ -203,18 +202,40 @@ def tile_fgg_pa_kernel(tc, x, adjacency_matrix, W1, b1, Wr1, out):
                 xgrp[tau // 2] = new_grp()
             words_out(eng, xgrp[tau // 2], tau % 2, xbank[tau])
 
-        def qx(i):
-            pair = quantise(xgrp[i], "x%d" % i)
-            xq[2 * i] = (pair, 0)
-            xq[2 * i + 1] = (pair, 256)
+        def qx(j, first=0, count=2):
+            c, s = xpair[j]
+            cols = slice(256 * first, 256 * (first + count))
+            V.quantize_mx(
+                out=c[:, cols].bitcast(FP8X4),
+                scales=s[:, cols],
+                in_=xgrp[j][:, 1024 * first : 1024 * (first + count)],
+            )
 
-        def qx_one(tau):
-            xq[tau] = (quantise(xgrp[tau // 2], "xt%d" % tau, 1024 * (tau % 2), 1024), 0)
+        def deal(j):
+            c, s = xpair[j]
+            V.tensor_copy(
+                out=xv_c[:, :, 32 * j : 32 * j + 32].bitcast(I32).rearrange("p (d o) i -> p o d i", o=4),
+                in_=c[:].bitcast(I32).rearrange("p (o d i) -> p o d i", o=4, d=4),
+            )
+            V.tensor_copy(
+                out=xv_s[:, :, 32 * j : 32 * j + 32].bitcast(I32).rearrange("p (d o) i -> p o d i", o=4),
+                in_=s[:].bitcast(I32).rearrange("p (o d i) -> p o d i", o=4, d=4),
+            )
+
+        def xq(tau, g):
+            return xpair[tau // 2], 256 * (tau % 2) + 128 * g
+
+        xv = (xv_c[:].rearrange("p s i -> p (s i)"), xv_s[:].rearrange("p s i -> p (s i)"))
+
+        def nodes(e, G, t, g):
+            if e == 1 and G < 2:
+                return xv, 128 * (4 * (2 * (t // 2) + G) + 2 * (t % 2) + g)
+            return xq(4 * G + t, g)
 
         def sup_group(e, G, c, t):
-            tau = 4 * G + t
             for g in range(2):
-                mx(sbank[(e, G, c)][:, t, :], xq[tau][0], xq[tau][1] + 128 * g, wq[(e, g)], 128 * c, P, g == 0, g == 1)
+                lt, col = nodes(e, G, t, g)
+                mx(sbank[(e, G, c)][:, t, :], lt, col, wq[(e, g)], 128 * c, P, g == 0, g == 1)
 
         def sup(e, G, c):
             sbank[(e, G, c)] = new_bank([P, 4, P])
@@ -233,180 +254,170 @@ def tile_fgg_pa_kernel(tc, x, adjacency_matrix, W1, b1, Wr1, out):
         def qs(e, G):
             sq[(e, G)] = quantise(sgrp[(e, G)], "s%d%d" % (e, G))
 
-        def ta(u, b):
+        def ta(kind, u, o):
+            w = araw[(kind, u)][:].bitcast(F32)
             bank = new_bank([P, 2, 2, P])
-            for o2 in range(2):
-                o = 2 * b + o2
-                if u in VU:
-                    q, e, G, row = o // 4, (o % 4) // 2, o % 2, 512
-                else:
-                    q, e, G, row = o // 6, (o % 6) // 3, o % 3, 768
-                w = araw[(e, u)][:].bitcast(F32)
+            for i in range(2):
                 for u2 in range(2):
-                    c0 = row * q + 256 * G + 128 * u2
-                    nc.tensor.transpose(out=bank[:, o2, u2, :], in_=w[:, c0 : c0 + P], identity=ident[:])
-            abank[(u, b)] = bank
+                    c0 = 512 * o + 256 * i + 128 * u2
+                    nc.tensor.transpose(out=bank[:, i, u2, :], in_=w[:, c0 : c0 + P], identity=ident[:])
+            abank[(kind, u, o)] = bank
+
+        def ca(kind, u, o, eng):
+            if o == 0:
+                agrp[(kind, u)] = new_grp()
+            words_out(eng, agrp[(kind, u)], o, abank[(kind, u, o)])
 
         def vt(u):
-            grp = new_grp()
-            for q in range(2):
-                for e in range(2):
-                    V.transpose(
-                        out=grp[:].bitcast(F32)[:, 256 * (2 * q + e) : 256 * (2 * q + e) + 256],
-                        in_=zt[(u, q, e)][:].bitcast(F32)[:, 256 * (u % 2) : 256 * (u % 2) + 256],
-                    )
-            agrp[(u, 2)] = grp
+            t = turn.tile([P, 1024], F32, name="turned", tag="turned", align_bytes=64)
+            V.transpose(out=t[:], in_=araw[("z", u)][:].bitcast(F32))
+            araw[("t", u)] = t
+
+        def cz(u, h, eng):
+            if h == 0:
+                agrp[("z", u)] = new_grp()
+            copy_on(
+                eng,
+                agrp[("z", u)][:].bitcast(F32)[:, 512 * h : 512 * h + 512].rearrange("p (b r v) -> p b r v", r=32, v=2),
+                araw[("t", u)][:].rearrange("p (b v k r) -> p k b r v", v=2, k=2, r=32)[:, h],
+            )
+
+        def qa(kind, u):
+            c = adjp.tile([P, 512], U32, name="c_" + kind, align_bytes=64)
+            s = adjp.tile([P, 512], U8, name="s_" + kind, align_bytes=64)
+            V.quantize_mx(out=c[:].bitcast(FP8X4), scales=s[:], in_=agrp[(kind, u)][:])
+            aq[(kind, u)] = (c, s)
 
         def operand(u, q, e, G):
-            if u not in VU:
-                o = 6 * q + 3 * e + G
-            elif G < 2:
-                o = 4 * q + 2 * e + G
-            else:
-                o = 8 + 2 * q + e
-            return (aq[(u, o // 4)], 128 * (o % 4))
+            if G == 2:
+                return aq[("g", u)], 128 * (2 * e + q)
+            if e == 1:
+                return aq[("z", u)], 128 * (2 * G + q)
+            return aq[("r", u)], 128 * (2 * q + G)
 
-        def ca(u, b, eng):
-            if b % 2 == 0:
-                agrp[(u, b // 2)] = new_grp()
-            words_out(eng, agrp[(u, b // 2)], b % 2, abank[(u, b)])
-
-        def qa(u, h):
-            aq[(u, h)] = quantise(agrp[(u, h)], "a%d%d" % (u, h))
-
-        def out_tile(u, q):
+        def out_cols(u, q, acc, lo, n):
             tau = 2 * u + q
-            acc = new_bank([P, 512])
             for g in range(2):
-                mx(acc[:], xq[tau][0], xq[tau][1] + 128 * g, wq[(2, g)], 0, 512, g == 0, False)
-            for e in range(2):
-                for G in range(3):
-                    lt = operand(u, q, e, G)
-                    mx(acc[:], lt[0], lt[1], sq[(e, G)], 0, 512, False, e == 1 and G == 2)
-            return acc
+                lt, col = xq(tau, g)
+                mx(acc, lt, col, wq[(2, g)], lo, n, g == 0, False)
+            for e, G in ((0, 0), (0, 1), (0, 2), (1, 0), (1, 1), (1, 2)):
+                lt, col = operand(u, q, e, G)
+                mx(acc, lt, col, sq[(e, G)], lo, n, False, (e, G) == (1, 2))
 
-        def out_half(u, q, acc, half):
-            tau = 2 * u + q
-            dst = acc[:]
-            for g in range(2):
-                mx(dst, xq[tau][0], xq[tau][1] + 128 * g, wq[(2, g)], 256 * half, 256, g == 0, False)
-            for e in range(2):
-                for G in range(3):
-                    lt = operand(u, q, e, G)
-                    mx(dst, lt[0], lt[1], sq[(e, G)], 256 * half, 256, False, e == 1 and G == 2)
-
-        def ev_half(u, q, acc, half):
-            cols = slice(256 * half, 256 * half + 256)
-            osb = outp.tile([P, 256], F32, name="osh", tag="osh", bufs=2)
-            V.tensor_tensor(out=osb[:], in0=acc[:], in1=bias_f[:, cols], op=ADD)
-            nc.sync.dma_start(out=out_v[u, q][:, cols], in_=osb[:])
-
-        def ev(u, q, acc):
+        def ev(u, q, acc, lo, n):
             osb = outp.tile([P, 512], F32, name="osb", tag="osb")
-            V.tensor_tensor(out=osb[:], in0=acc[:], in1=bias_f[:], op=ADD)
-            nc.sync.dma_start(out=out_v[u, q], in_=osb[:])
+            V.tensor_tensor(out=osb[:, 0:n], in0=acc, in1=bias_f[:, lo : lo + n], op=ADD)
+            nc.sync.dma_start(out=out_v[u, q][:, lo : lo + n], in_=osb[:, 0:n])
 
-        def s_block(e, G, vshare, before=None):
+        def out_tile(u, q, n=512):
+            for lo in range(0, 512, n):
+                acc = new_bank([P, n])
+                out_cols(u, q, acc[:], lo, n)
+                ev(u, q, acc[:], lo, n)
+
+        def s_block(e, G, vc=(3,)):
             for c in range(4):
                 sup(e, G, c)
-            if before is not None:
-                qs(before[0], before[1])
             for c in range(4):
-                cs(e, G, c, V if (vshare and c == 3) else S)
+                cs(e, G, c, V if c in vc else S)
+
+        def t_rows(u, engs):
+            for o in range(2):
+                ta("r", u, o)
+            for o in range(2):
+                ta("g", u, o)
+            for o in range(2):
+                ca("r", u, o, engs[o])
+            for o in range(2):
+                ca("g", u, o, engs[2 + o])
 
         warm(10)
+        for tau in range(8):
+            tx(tau)
         rw(0, 0)
         rw(0, 1)
+        for tau in range(4):
+            cx(tau, S)
         qw(0, 0)
         qw(0, 1)
-        for tau in range(4):
-            tx(tau)
+        qx(0)
+        qx(1)
         for c in range(4):
-            sbank[(0, 0, c)] = new_bank([P, 4, P])
-        for tau in range(4):
-            cx(tau, S)
-            qx_one(tau)
-            for c in range(4):
-                sup_group(0, 0, c, tau)
-        pump(3)
-        rw(1, 0)
-        rw(1, 1)
-        qw(1, 0)
-        qw(1, 1)
-        pump(5)
-        for c in range(4):
-            cs(0, 0, c, S)
-        for tau in range(4, 8):
-            tx(tau)
+            sup(0, 0, c)
         for tau in range(4, 8):
             cx(tau, S)
-        qs(0, 0)
+        deal(0)
+        deal(1)
         qx(2)
         qx(3)
-        pump(7)
-        s_block(1, 0, False)
+        rw(1, 0, 128)
+        rw(1, 1, 128)
+        for c in range(4):
+            cs(0, 0, c, S)
+        for c in range(4):
+            sup(0, 1, c)
+        qw(1, 0)
+        qw(1, 1)
+
+        deal(2)
+        deal(3)
+        qs(0, 0)
+        for c in range(4):
+            cs(0, 1, c, S)
         for tau in range(8, 12):
             tx(tau)
+        qs(0, 1)
         for tau in range(8, 12):
             cx(tau, S)
-        rw(2, 0)
-        rw(2, 1)
-        qw(2, 0)
-        qw(2, 1)
-        bias_bank = new_bank([P, 512])
-        nc.tensor.matmul(out=bias_bank[:], lhsT=ones[:], rhs=bias_row[:], start=True, stop=True)
-        S.copy(out=bias_f[:], in_=bias_bank[:])
-        pump(11)
-        qs(1, 0)
+        pump(9)
         qx(4)
         qx(5)
-        s_block(0, 1, True)
-        s_block(1, 1, True, (0, 1))
-
-        def t_unit(u, vbanks):
-            for b in range(6):
-                ta(u, b)
-                ca(u, b, V if b in vbanks else S)
-                if b == 4:
-                    qa(u, 0)
-            qa(u, 1)
-            qa(u, 2)
-
-        def t_short(u):
-            for b in range(4):
-                ta(u, b)
-                ca(u, b, S)
-
-        VBA = (2, 5)
+        for e, G in ((1, 0), (1, 1)):
+            for c in range(4):
+                sup(e, G, c)
+            for c in range(4):
+                cs(e, G, c, V if c == 3 else S)
+            if (e, G) == (1, 0):
+                rw(2, 0, 128)
+                rw(2, 1, 128)
+            if (e, G) == (1, 1):
+                qs(1, 0)
+                qw(2, 0)
+                qw(2, 1)
+        pump(12)
+        t_rows(0, (S, S, S, S))
+        vt(0)
+        for c in range(4):
+            sup(0, 2, c)
         qs(1, 1)
-        t_unit(0, VBA)
-        s_block(0, 2, True)
-        s_block(1, 2, True, (0, 2))
+        qa("r", 0)
+        for c in range(4):
+            cs(0, 2, c, V if c == 3 else S)
+        pump(13)
+        qa("g", 0)
+        for c in range(4):
+            sup(1, 2, c)
+        cz(0, 0, S)
+        cz(0, 1, V)
+        qs(0, 2)
+        for c in range(4):
+            cs(1, 2, c, V if c == 3 else S)
+        qa("z", 0)
+        t_rows(1, (S, S, S, S))
         qs(1, 2)
-        t_unit(1, VBA)
-        for q in range(2):
-            ev(0, q, out_tile(0, q))
-        t_unit(2, (5,))
-        t_unit(3, (5,))
-        for u in (1, 2):
+        V.tensor_copy(out=bias_f[:], in_=bias_bf[:])
+        vt(1)
+        pump(15)
+        for u in range(6):
             for q in range(2):
-                ev(u, q, out_tile(u, q))
-        t_short(4)
-        t_short(5)
-        qa(4, 0)
-        qa(4, 1)
-        vt(4)
-        qa(5, 0)
-        qa(4, 2)
-        qa(5, 1)
-        for q in range(2):
-            ev(3, q, out_tile(3, q))
-        vt(5)
-        ev(4, 0, out_tile(4, 0))
-        qa(5, 2)
-        ev(4, 1, out_tile(4, 1))
-        ev(5, 0, out_tile(5, 0))
-        for half in range(2):
-            last = new_bank([P, 256])
-            out_half(5, 1, last, half)
-            ev_half(5, 1, last, half)
+                out_tile(u, q, 256 if (u, q) == (5, 1) else 512)
+                if q == 0 and u < 5:
+                    qa("r", u + 1)
+                    qa("g", u + 1)
+                    cz(u + 1, 0, S)
+                    cz(u + 1, 1, S)
+                    qa("z", u + 1)
+            if u < 4:
+                t_rows(u + 2, (S, S, S, S))
+                vt(u + 2)
+                pump(17 + 2 * u)

@@ -22,7 +22,7 @@ def tile_fgg_pa_kernel(tc, x, adjacency_matrix, W1, b1, Wr1, out):
     out_v = out.rearrange("(j p e) f -> j e p f", p=P, e=2)
     with ExitStack() as ctx:
         const = ctx.enter_context(tc.tile_pool(name="const", bufs=1))
-        rawp = ctx.enter_context(tc.tile_pool(name="rawp", bufs=16))
+        rawp = ctx.enter_context(tc.tile_pool(name="rawp", bufs=20))
         grpp = ctx.enter_context(tc.tile_pool(name="grpp", bufs=8))
         turn = ctx.enter_context(tc.tile_pool(name="turn", bufs=3))
         keep = ctx.enter_context(tc.tile_pool(name="keep", bufs=1))
@@ -72,7 +72,11 @@ def tile_fgg_pa_kernel(tc, x, adjacency_matrix, W1, b1, Wr1, out):
         V.memset(zeros[:], 0.0)
         ident = const.tile([P, P], F32, name="ident")
         make_identity(nc, ident[:])
-        bias_bf = const.tile([P, 512], BF16, name="bias_bf")
+        bias_row = const.tile([P, 512], BF16, name="bias_row")
+        V.memset(bias_row[:], 0.0)
+        nc.scalar.dma_start(out=bias_row[0:1, :], in_=b1.unsqueeze(0))
+        ones = const.tile([P, P], BF16, name="ones")
+        V.memset(ones[:], 1.0)
         bias_f = const.tile([P, 512], F32, name="bias_f")
         xpair = {}
         for j in range(6):
@@ -106,7 +110,7 @@ def tile_fgg_pa_kernel(tc, x, adjacency_matrix, W1, b1, Wr1, out):
             t = new_raw()
             z = t[:].rearrange("p (q b m) -> p q b m", q=2, b=4)
             for q in range(2):
-                for a in range(4):
+                for a in (0, 2, 1, 3):
                     nc.sync.dma_start(
                         out=z[32 * a : 32 * a + 32, q],
                         in_=adj_r[1, u, q][:, :, 256 * a : 256 * a + 256],
@@ -147,8 +151,7 @@ def tile_fgg_pa_kernel(tc, x, adjacency_matrix, W1, b1, Wr1, out):
         load_x(5)
         load_w(2, Wr1, 0)
         load_w(2, Wr1, 1)
-        nc.sync.dma_start(out=bias_bf[:], in_=b1.partition_broadcast(P))
-        pump(16 - 12)
+        pump(8)
 
         wgrp = {}
         wq = {}
@@ -369,7 +372,7 @@ def tile_fgg_pa_kernel(tc, x, adjacency_matrix, W1, b1, Wr1, out):
         qs(0, 1)
         for tau in range(8, 12):
             cx(tau, S)
-        pump(9)
+        pump(18)
         qx(4)
         qx(5)
         for e, G in ((1, 0), (1, 1)):
@@ -384,7 +387,6 @@ def tile_fgg_pa_kernel(tc, x, adjacency_matrix, W1, b1, Wr1, out):
                 qs(1, 0)
                 qw(2, 0)
                 qw(2, 1)
-        pump(12)
         t_rows(0, (S, S, S, S))
         vt(0)
         for c in range(4):
@@ -393,7 +395,6 @@ def tile_fgg_pa_kernel(tc, x, adjacency_matrix, W1, b1, Wr1, out):
         qa("r", 0)
         for c in range(4):
             cs(0, 2, c, V if c == 3 else S)
-        pump(13)
         qa("g", 0)
         for c in range(4):
             sup(1, 2, c)
@@ -405,19 +406,19 @@ def tile_fgg_pa_kernel(tc, x, adjacency_matrix, W1, b1, Wr1, out):
         qa("z", 0)
         t_rows(1, (S, S, S, S))
         qs(1, 2)
-        V.tensor_copy(out=bias_f[:], in_=bias_bf[:])
-        vt(1)
-        pump(15)
+        bias_bank = new_bank([P, 512])
+        nc.tensor.matmul(out=bias_bank[:], lhsT=ones[:], rhs=bias_row[:], start=True, stop=True)
+        S.copy(out=bias_f[:], in_=bias_bank[:])
         for u in range(6):
+            if u < 5:
+                vt(u + 1)
+                qa("r", u + 1)
+                qa("g", u + 1)
+                cz(u + 1, 0, S)
+                cz(u + 1, 1, S)
             for q in range(2):
                 out_tile(u, q, 256 if (u, q) == (5, 1) else 512)
                 if q == 0 and u < 5:
-                    qa("r", u + 1)
-                    qa("g", u + 1)
-                    cz(u + 1, 0, S)
-                    cz(u + 1, 1, S)
                     qa("z", u + 1)
             if u < 4:
                 t_rows(u + 2, (S, S, S, S))
-                vt(u + 2)
-                pump(17 + 2 * u)

@@ -132,8 +132,11 @@ def tile_fgg_pa_kernel(tc, x, adjacency_matrix, W1, b1, Wr1, out):
             araw[("g", u)] = t
 
         queue = []
-        for u in range(6):
-            queue.extend([(load_rows, u), (load_last, u), (load_blocks, u)])
+        for us in ((0,), (1,), (2, 3), (4, 5)):
+            for u in us:
+                queue.extend([(load_rows, u), (load_last, u)])
+            for u in us:
+                queue.append((load_blocks, u))
 
         def pump(count):
             while state["next"] < min(count, len(queue)):
@@ -324,19 +327,30 @@ def tile_fgg_pa_kernel(tc, x, adjacency_matrix, W1, b1, Wr1, out):
             for c in range(4):
                 cs(e, G, c, V if c in vc else S)
 
-        def t_rows(u, engs):
-            for o in range(2):
-                ta("r", u, o)
-            for o in range(2):
-                ta("g", u, o)
-            for o in range(2):
-                ca("r", u, o, engs[o])
-            for o in range(2):
-                ca("g", u, o, engs[2 + o])
+        def turn_rows(u):
+            for kind in ("r", "g"):
+                for o in range(2):
+                    ta(kind, u, o)
 
-        warm(10)
+        def prepare(u, last=S):
+            vt(u)
+            for kind in ("r", "g"):
+                for o in range(2):
+                    ca(kind, u, o, S)
+                qa(kind, u)
+            cz(u, 0, S)
+            cz(u, 1, last)
+            qa("z", u)
+
+        warm(6)
+        bias_bank = psum.tile([P, 512], F32, name="bank6", tag="bank6")
+        nc.tensor.matmul(out=bias_bank[:], lhsT=ones[:], rhs=bias_row[:], start=True, stop=True)
+        S.copy(out=bias_f[:], in_=bias_bank[:])
+        warm(3)
         for tau in range(8):
             tx(tau)
+            if tau in (1, 3, 5):
+                warm(1)
         rw(0, 0)
         rw(0, 1)
         for tau in range(4):
@@ -353,7 +367,7 @@ def tile_fgg_pa_kernel(tc, x, adjacency_matrix, W1, b1, Wr1, out):
         deal(1)
         qx(2)
         qx(3)
-        rw(1, 0, 128)
+        rw(1, 0, 0)
         rw(1, 1, 128)
         for c in range(4):
             cs(0, 0, c, S)
@@ -371,7 +385,7 @@ def tile_fgg_pa_kernel(tc, x, adjacency_matrix, W1, b1, Wr1, out):
             tx(tau)
         qs(0, 1)
         for tau in range(8, 12):
-            cx(tau, S)
+            cx(tau, V if tau == 11 else S)
         pump(18)
         qx(4)
         qx(5)
@@ -387,8 +401,11 @@ def tile_fgg_pa_kernel(tc, x, adjacency_matrix, W1, b1, Wr1, out):
                 qs(1, 0)
                 qw(2, 0)
                 qw(2, 1)
-        t_rows(0, (S, S, S, S))
+        turn_rows(0)
         vt(0)
+        for kind in ("r", "g"):
+            for o in range(2):
+                ca(kind, 0, o, S)
         for c in range(4):
             sup(0, 2, c)
         qs(1, 1)
@@ -404,21 +421,14 @@ def tile_fgg_pa_kernel(tc, x, adjacency_matrix, W1, b1, Wr1, out):
         for c in range(4):
             cs(1, 2, c, V if c == 3 else S)
         qa("z", 0)
-        t_rows(1, (S, S, S, S))
+        turn_rows(1)
         qs(1, 2)
-        bias_bank = new_bank([P, 512])
-        nc.tensor.matmul(out=bias_bank[:], lhsT=ones[:], rhs=bias_row[:], start=True, stop=True)
-        S.copy(out=bias_f[:], in_=bias_bank[:])
+        prepare(1)
         for u in range(6):
-            if u < 5:
-                vt(u + 1)
-                qa("r", u + 1)
-                qa("g", u + 1)
-                cz(u + 1, 0, S)
-                cz(u + 1, 1, S)
             for q in range(2):
                 out_tile(u, q, 256 if (u, q) == (5, 1) else 512)
-                if q == 0 and u < 5:
-                    qa("z", u + 1)
-            if u < 4:
-                t_rows(u + 2, (S, S, S, S))
+            if u in (0, 2):
+                turn_rows(u + 2)
+                turn_rows(u + 3)
+                prepare(u + 2)
+                prepare(u + 3)

@@ -22,7 +22,8 @@ def tile_fgg_pa_kernel(tc, x, adjacency_matrix, W1, b1, Wr1, out):
     out_v = out.rearrange("(j p e) f -> j e p f", p=P, e=2)
     with ExitStack() as ctx:
         const = ctx.enter_context(tc.tile_pool(name="const", bufs=1))
-        rawp = ctx.enter_context(tc.tile_pool(name="rawp", bufs=20))
+        rawp = ctx.enter_context(tc.tile_pool(name="rawp", bufs=13))
+        rowp = ctx.enter_context(tc.tile_pool(name="rowp", bufs=4))
         grpp = ctx.enter_context(tc.tile_pool(name="grpp", bufs=8))
         turn = ctx.enter_context(tc.tile_pool(name="turn", bufs=3))
         keep = ctx.enter_context(tc.tile_pool(name="keep", bufs=1))
@@ -68,13 +69,12 @@ def tile_fgg_pa_kernel(tc, x, adjacency_matrix, W1, b1, Wr1, out):
                 stop=stop,
             )
 
+        bias_row = const.tile([P, 512], BF16, name="bias_row")
         zeros = const.tile([P, 512], BF16, name="zeros")
         V.memset(zeros[:], 0.0)
+        V.memset(bias_row[:], 0.0)
         ident = const.tile([P, P], F32, name="ident")
         make_identity(nc, ident[:])
-        bias_row = const.tile([P, 512], BF16, name="bias_row")
-        V.memset(bias_row[:], 0.0)
-        nc.scalar.dma_start(out=bias_row[0:1, :], in_=b1.unsqueeze(0))
         ones = const.tile([P, P], BF16, name="ones")
         V.memset(ones[:], 1.0)
         bias_f = const.tile([P, 512], F32, name="bias_f")
@@ -118,17 +118,13 @@ def tile_fgg_pa_kernel(tc, x, adjacency_matrix, W1, b1, Wr1, out):
             araw[("z", u)] = t
 
         def load_rows(u):
-            t = new_raw()
-            nc.sync.dma_start(out=t[:].rearrange("p (q m) -> p q m", q=2), in_=adj_q[0, u][:, :, 0:1024])
+            t = rowp.tile([P, 3072], BF16, name="rows", tag="rows", align_bytes=64)
+            nc.sync.dma_start(out=t[:], in_=adj_q[0, u].rearrange("p q m -> p (q m)"))
             araw[("r", u)] = t
 
         def load_last(u):
-            t = new_raw()
-            for e in range(2):
-                nc.sync.dma_start(
-                    out=t[:, 1024 * e : 1024 * e + 1024].rearrange("p (q m) -> p q m", q=2),
-                    in_=adj_q[e, u][:, :, 1024:1536],
-                )
+            t = rowp.tile([P, 1024], BF16, name="last", tag="last", align_bytes=64)
+            nc.sync.dma_start(out=t[:].rearrange("p (q m) -> p q m", q=2), in_=adj_q[1, u][:, :, 1024:1536])
             araw[("g", u)] = t
 
         queue = []
@@ -146,6 +142,7 @@ def tile_fgg_pa_kernel(tc, x, adjacency_matrix, W1, b1, Wr1, out):
 
         load_w(0, W1[0], 0)
         load_w(0, W1[0], 1)
+        nc.sync.dma_start(out=bias_row[0:1, :], in_=b1.unsqueeze(0))
         for j in range(4):
             load_x(j)
         load_w(1, W1[1], 0)
@@ -154,7 +151,7 @@ def tile_fgg_pa_kernel(tc, x, adjacency_matrix, W1, b1, Wr1, out):
         load_x(5)
         load_w(2, Wr1, 0)
         load_w(2, Wr1, 1)
-        pump(8)
+        pump(5)
 
         wgrp = {}
         wq = {}
@@ -260,13 +257,21 @@ def tile_fgg_pa_kernel(tc, x, adjacency_matrix, W1, b1, Wr1, out):
         def qs(e, G):
             sq[(e, G)] = quantise(sgrp[(e, G)], "s%d%d" % (e, G))
 
+        def words(kind, u, o, i):
+            if kind == "r":
+                return araw[("r", u)][:].bitcast(F32), 768 * o + 256 * i
+            if o == 0:
+                return araw[("r", u)][:].bitcast(F32), 768 * i + 512
+            return araw[("g", u)][:].bitcast(F32), 256 * i
+
         def ta(kind, u, o):
-            w = araw[(kind, u)][:].bitcast(F32)
             bank = new_bank([P, 2, 2, P])
             for i in range(2):
+                w, c0 = words(kind, u, o, i)
                 for u2 in range(2):
-                    c0 = 512 * o + 256 * i + 128 * u2
-                    nc.tensor.transpose(out=bank[:, i, u2, :], in_=w[:, c0 : c0 + P], identity=ident[:])
+                    nc.tensor.transpose(
+                        out=bank[:, i, u2, :], in_=w[:, c0 + 128 * u2 : c0 + 128 * u2 + P], identity=ident[:]
+                    )
             abank[(kind, u, o)] = bank
 
         def ca(kind, u, o, eng):
@@ -342,11 +347,10 @@ def tile_fgg_pa_kernel(tc, x, adjacency_matrix, W1, b1, Wr1, out):
             cz(u, 1, last)
             qa("z", u)
 
-        warm(6)
+        warm(9)
         bias_bank = psum.tile([P, 512], F32, name="bank6", tag="bank6")
         nc.tensor.matmul(out=bias_bank[:], lhsT=ones[:], rhs=bias_row[:], start=True, stop=True)
         S.copy(out=bias_f[:], in_=bias_bank[:])
-        warm(3)
         for tau in range(8):
             tx(tau)
             if tau in (1, 3, 5):
@@ -386,7 +390,7 @@ def tile_fgg_pa_kernel(tc, x, adjacency_matrix, W1, b1, Wr1, out):
         qs(0, 1)
         for tau in range(8, 12):
             cx(tau, V if tau == 11 else S)
-        pump(18)
+        pump(12)
         qx(4)
         qx(5)
         for e, G in ((1, 0), (1, 1)):
@@ -422,6 +426,7 @@ def tile_fgg_pa_kernel(tc, x, adjacency_matrix, W1, b1, Wr1, out):
             cs(1, 2, c, V if c == 3 else S)
         qa("z", 0)
         turn_rows(1)
+        pump(18)
         qs(1, 2)
         prepare(1)
         for u in range(6):

from contextlib import ExitStack

import concourse.mybir as mybir
from concourse.masks import make_identity

F32 = mybir.dt.float32
BF16 = mybir.dt.bfloat16
U32 = mybir.dt.uint32
I32 = mybir.dt.int32
U8 = mybir.dt.uint8
FP8X4 = mybir.dt.float8_e4m3fn_x4
ADD = mybir.AluOpType.add
P = 128
FLOPS = 9663676416


def tile_fgg_pa_kernel(tc, x, adjacency_matrix, W1, b1, Wr1, out):
    nc = tc.nc
    x_v = x.rearrange("(j p e) k -> j p (e k)", p=P, e=2)
    adj_q = adjacency_matrix.rearrange("a (j p q) m -> a j p q m", p=P, q=2)
    adj_r = adjacency_matrix.rearrange("a (j b r q) m -> a j q r b m", b=4, r=32, q=2)
    out_v = out.rearrange("(j p e) f -> j e p f", p=P, e=2)
    with ExitStack() as ctx:
        const = ctx.enter_context(tc.tile_pool(name="const", bufs=1))
        rawp = ctx.enter_context(tc.tile_pool(name="rawp", bufs=13))
        rowp = ctx.enter_context(tc.tile_pool(name="rowp", bufs=4))
        grpp = ctx.enter_context(tc.tile_pool(name="grpp", bufs=8))
        turn = ctx.enter_context(tc.tile_pool(name="turn", bufs=3))
        keep = ctx.enter_context(tc.tile_pool(name="keep", bufs=1))
        adjp = ctx.enter_context(tc.tile_pool(name="adjp", bufs=4))
        outp = ctx.enter_context(tc.tile_pool(name="outp", bufs=6))
        psum = ctx.enter_context(tc.psum_pool(name="psum", bufs=1))
        ctx.enter_context(tc.manual_schedule())
        state = {"bank": 0, "next": 0}
        V = nc.vector
        S = nc.scalar

        def new_bank(shape):
            i = state["bank"]
            state["bank"] = i + 1
            return psum.tile(shape, F32, name="bank%d" % (i % 8), tag="bank%d" % (i % 8))

        def new_raw():
            return rawp.tile([P, 2048], BF16, name="raw", tag="raw", align_bytes=64)

        def new_grp():
            return grpp.tile([P, 2048], BF16, name="grp", tag="grp", align_bytes=64)

        def copy_on(eng, dst, src):
            if eng is S:
                S.copy(out=dst, in_=src)
            else:
                V.tensor_copy(out=dst, in_=src)

        def quantise(grp, nm, lo=0, width=2048, pool=keep, filled=False):
            c = pool.tile([P, width // 4], U32, name="c_" + nm, align_bytes=64)
            s = pool.tile([P, width // 4], U8, name="s_" + nm, align_bytes=64)
            V.quantize_mx(out=c[:].bitcast(FP8X4), scales=s[:], in_=grp[:, lo : lo + width])
            return (c, s)

        def mx(acc, lt, lcol, rt, rcol, n, start, stop):
            nc.tensor.matmul_mx(
                out=acc,
                lhsT=lt[0][:, lcol : lcol + P].bitcast(FP8X4),
                lhsT_scale=lt[1][:, lcol : lcol + P],
                rhs=rt[0][:, rcol : rcol + n].bitcast(FP8X4),
                rhs_scale=rt[1][:, rcol : rcol + n],
                start=start,
                stop=stop,
            )

        bias_row = const.tile([P, 512], BF16, name="bias_row")
        zeros = const.tile([P, 512], BF16, name="zeros")
        V.memset(zeros[:], 0.0)
        V.memset(bias_row[:], 0.0)
        ident = const.tile([P, P], F32, name="ident")
        make_identity(nc, ident[:])
        ones = const.tile([P, P], BF16, name="ones")
        V.memset(ones[:], 1.0)
        bias_f = const.tile([P, 512], F32, name="bias_f")
        xpair = {}
        for j in range(6):
            c = keep.tile([P, 512], U32, name="c_x%d" % j, align_bytes=64)
            s = keep.tile([P, 512], U8, name="s_x%d" % j, align_bytes=64)
            if j < 4:
                nc.gpsimd.memset(s[:].bitcast(U32), 0)
            xpair[j] = (c, s)
        xv_c = keep.tile([P, 16, P], U32, name="xv_c", align_bytes=64)
        xv_s = keep.tile([P, 16, P], U8, name="xv_s", align_bytes=64)

        xraw = {}
        wraw = {}
        araw = {}

        def load_x(j, halves=(0, 1)):
            if 0 in halves:
                xraw[j] = new_raw()
            cols = slice(1024 * halves[0], 1024 * halves[-1] + 1024)
            nc.sync.dma_start(out=xraw[j][:, cols], in_=x_v[j][:, cols])

        def load_w(key, src, g):
            t = new_raw()
            nc.sync.dma_start(
                out=t[:].rearrange("p (u r) -> p u r", u=2),
                in_=src[512 * g : 512 * g + 512, :].rearrange("(u p q) c -> p u (q c)", u=2, p=P, q=2),
            )
            wraw[(key, g)] = t

        def load_blocks(u):
            t = new_raw()
            z = t[:].rearrange("p (q b m) -> p q b m", q=2, b=4)
            for q in range(2):
                for a in (0, 2, 1, 3):
                    nc.sync.dma_start(
                        out=z[32 * a : 32 * a + 32, q],
                        in_=adj_r[1, u, q][:, :, 256 * a : 256 * a + 256],
                    )
            araw[("z", u)] = t

        def load_rows(u):
            t = rowp.tile([P, 3072], BF16, name="rows", tag="rows", align_bytes=64)
            nc.sync.dma_start(out=t[:], in_=adj_q[0, u].rearrange("p q m -> p (q m)"))
            araw[("r", u)] = t

        def load_last(u):
            t = rowp.tile([P, 1024], BF16, name="last", tag="last", align_bytes=64)
            nc.sync.dma_start(out=t[:].rearrange("p (q m) -> p q m", q=2), in_=adj_q[1, u][:, :, 1024:1536])
            araw[("g", u)] = t

        queue = []
        for us in ((0,), (1,), (2, 3), (4, 5)):
            for u in us:
                queue.extend([(load_rows, u), (load_last, u)])
            for u in us:
                queue.append((load_blocks, u))

        def pump(count):
            while state["next"] < min(count, len(queue)):
                fn, u = queue[state["next"]]
                fn(u)
                state["next"] = state["next"] + 1

        load_w(0, W1[0], 0)
        load_w(0, W1[0], 1)
        nc.sync.dma_start(out=bias_row[0:1, :], in_=b1.unsqueeze(0))
        for j in range(4):
            load_x(j)
        load_w(1, W1[1], 0)
        load_w(1, W1[1], 1)
        load_x(4)
        load_x(5)
        load_w(2, Wr1, 0)
        load_w(2, Wr1, 1)
        pump(5)

        wgrp = {}
        wq = {}
        xbank = {}
        xgrp = {}
        sbank = {}
        sgrp = {}
        sq = {}
        abank = {}
        agrp = {}
        aq = {}

        def warm(count):
            bank = psum.tile([P, 512], F32, name="bank7", tag="bank7")
            for i in range(count):
                nc.tensor.matmul(out=bank[:], lhsT=zeros[:, 0:P], rhs=zeros[:], start=True, stop=True)

        def rw(key, g, scalar_cols=0):
            grp = new_grp()
            cut = (512 - scalar_cols) // 4
            for eng, lo, hi in ((V, 0, cut), (S, cut, 128)):
                if lo < hi:
                    copy_on(
                        eng,
                        grp[:].rearrange("p (c i t) -> p c t i", i=4, t=4)[:, lo:hi],
                        wraw[(key, g)][:].rearrange("p (t c i) -> p c t i", t=4, i=4)[:, lo:hi],
                    )
            wgrp[(key, g)] = grp

        def qw(key, g):
            wq[(key, g)] = quantise(wgrp[(key, g)], "w%d%d" % (key, g))

        def tx(tau):
            w = xraw[tau // 2][:].bitcast(F32)
            bank = new_bank([P, 2, 2, P])
            for g in range(2):
                for u in range(2):
                    c0 = 512 * (tau % 2) + 256 * g + 128 * u
                    nc.tensor.transpose(out=bank[:, g, u, :], in_=w[:, c0 : c0 + P], identity=ident[:])
            xbank[tau] = bank

        def words_out(eng, grp, half, bank):
            copy_on(
                eng,
                grp[:].bitcast(F32)[:, 512 * half : 512 * half + 512].rearrange("p (o n u) -> p o n u", o=2, n=P, u=2),
                bank[:].rearrange("p o u n -> p o n u"),
            )

        def cx(tau, eng):
            if tau % 2 == 0:
                xgrp[tau // 2] = new_grp()
            words_out(eng, xgrp[tau // 2], tau % 2, xbank[tau])

        def qx(j, first=0, count=2):
            c, s = xpair[j]
            cols = slice(256 * first, 256 * (first + count))
            V.quantize_mx(
                out=c[:, cols].bitcast(FP8X4),
                scales=s[:, cols],
                in_=xgrp[j][:, 1024 * first : 1024 * (first + count)],
            )

        def deal(j):
            c, s = xpair[j]
            V.tensor_copy(
                out=xv_c[:, :, 32 * j : 32 * j + 32].bitcast(I32).rearrange("p (d o) i -> p o d i", o=4),
                in_=c[:].bitcast(I32).rearrange("p (o d i) -> p o d i", o=4, d=4),
            )
            V.tensor_copy(
                out=xv_s[:, :, 32 * j : 32 * j + 32].bitcast(I32).rearrange("p (d o) i -> p o d i", o=4),
                in_=s[:].bitcast(I32).rearrange("p (o d i) -> p o d i", o=4, d=4),
            )

        def xq(tau, g):
            return xpair[tau // 2], 256 * (tau % 2) + 128 * g

        xv = (xv_c[:].rearrange("p s i -> p (s i)"), xv_s[:].rearrange("p s i -> p (s i)"))

        def nodes(e, G, t, g):
            if e == 1 and G < 2:
                return xv, 128 * (4 * (2 * (t // 2) + G) + 2 * (t % 2) + g)
            return xq(4 * G + t, g)

        def sup_group(e, G, c, t):
            for g in range(2):
                lt, col = nodes(e, G, t, g)
                mx(sbank[(e, G, c)][:, t, :], lt, col, wq[(e, g)], 128 * c, P, g == 0, g == 1)

        def sup(e, G, c):
            sbank[(e, G, c)] = new_bank([P, 4, P])
            for t in range(4):
                sup_group(e, G, c, t)

        def cs(e, G, c, eng):
            if c == 0:
                sgrp[(e, G)] = new_grp()
            copy_on(
                eng,
                sgrp[(e, G)][:, 512 * c : 512 * c + 512].rearrange("p (f t) -> p f t", t=4),
                sbank[(e, G, c)][:].rearrange("p t f -> p f t"),
            )

        def qs(e, G):
            sq[(e, G)] = quantise(sgrp[(e, G)], "s%d%d" % (e, G))

        def words(kind, u, o, i):
            if kind == "r":
                return araw[("r", u)][:].bitcast(F32), 768 * o + 256 * i
            if o == 0:
                return araw[("r", u)][:].bitcast(F32), 768 * i + 512
            return araw[("g", u)][:].bitcast(F32), 256 * i

        def ta(kind, u, o):
            bank = new_bank([P, 2, 2, P])
            for i in range(2):
                w, c0 = words(kind, u, o, i)
                for u2 in range(2):
                    nc.tensor.transpose(
                        out=bank[:, i, u2, :], in_=w[:, c0 + 128 * u2 : c0 + 128 * u2 + P], identity=ident[:]
                    )
            abank[(kind, u, o)] = bank

        def ca(kind, u, o, eng):
            if o == 0:
                agrp[(kind, u)] = new_grp()
            words_out(eng, agrp[(kind, u)], o, abank[(kind, u, o)])

        def vt(u):
            t = turn.tile([P, 1024], F32, name="turned", tag="turned", align_bytes=64)
            V.transpose(out=t[:], in_=araw[("z", u)][:].bitcast(F32))
            araw[("t", u)] = t

        def cz(u, h, eng):
            if h == 0:
                agrp[("z", u)] = new_grp()
            copy_on(
                eng,
                agrp[("z", u)][:].bitcast(F32)[:, 512 * h : 512 * h + 512].rearrange("p (b r v) -> p b r v", r=32, v=2),
                araw[("t", u)][:].rearrange("p (b v k r) -> p k b r v", v=2, k=2, r=32)[:, h],
            )

        def qa(kind, u):
            c = adjp.tile([P, 512], U32, name="c_" + kind, align_bytes=64)
            s = adjp.tile([P, 512], U8, name="s_" + kind, align_bytes=64)
            V.quantize_mx(out=c[:].bitcast(FP8X4), scales=s[:], in_=agrp[(kind, u)][:])
            aq[(kind, u)] = (c, s)

        def operand(u, q, e, G):
            if G == 2:
                return aq[("g", u)], 128 * (2 * e + q)
            if e == 1:
                return aq[("z", u)], 128 * (2 * G + q)
            return aq[("r", u)], 128 * (2 * q + G)

        def out_cols(u, q, acc, lo, n):
            tau = 2 * u + q
            for g in range(2):
                lt, col = xq(tau, g)
                mx(acc, lt, col, wq[(2, g)], lo, n, g == 0, False)
            for e, G in ((0, 0), (0, 1), (0, 2), (1, 0), (1, 1), (1, 2)):
                lt, col = operand(u, q, e, G)
                mx(acc, lt, col, sq[(e, G)], lo, n, False, (e, G) == (1, 2))

        def ev(u, q, acc, lo, n):
            osb = outp.tile([P, 512], F32, name="osb", tag="osb")
            V.tensor_tensor(out=osb[:, 0:n], in0=acc, in1=bias_f[:, lo : lo + n], op=ADD)
            nc.sync.dma_start(out=out_v[u, q][:, lo : lo + n], in_=osb[:, 0:n])

        def out_tile(u, q, n=512):
            for lo in range(0, 512, n):
                acc = new_bank([P, n])
                out_cols(u, q, acc[:], lo, n)
                ev(u, q, acc[:], lo, n)

        def s_block(e, G, vc=(3,)):
            for c in range(4):
                sup(e, G, c)
            for c in range(4):
                cs(e, G, c, V if c in vc else S)

        def turn_rows(u):
            for kind in ("r", "g"):
                for o in range(2):
                    ta(kind, u, o)

        def prepare(u, last=S):
            vt(u)
            for kind in ("r", "g"):
                for o in range(2):
                    ca(kind, u, o, S)
                qa(kind, u)
            cz(u, 0, S)
            cz(u, 1, last)
            qa("z", u)

        warm(9)
        bias_bank = psum.tile([P, 512], F32, name="bank6", tag="bank6")
        nc.tensor.matmul(out=bias_bank[:], lhsT=ones[:], rhs=bias_row[:], start=True, stop=True)
        S.copy(out=bias_f[:], in_=bias_bank[:])
        for tau in range(8):
            tx(tau)
            if tau in (1, 3, 5):
                warm(1)
        rw(0, 0)
        rw(0, 1)
        for tau in range(4):
            cx(tau, S)
        qw(0, 0)
        qw(0, 1)
        qx(0)
        qx(1)
        for c in range(4):
            sup(0, 0, c)
        for tau in range(4, 8):
            cx(tau, S)
        deal(0)
        deal(1)
        qx(2)
        qx(3)
        rw(1, 0, 0)
        rw(1, 1, 128)
        for c in range(4):
            cs(0, 0, c, S)
        for c in range(4):
            sup(0, 1, c)
        qw(1, 0)
        qw(1, 1)

        deal(2)
        deal(3)
        qs(0, 0)
        for c in range(4):
            cs(0, 1, c, S)
        for tau in range(8, 12):
            tx(tau)
        qs(0, 1)
        for tau in range(8, 12):
            cx(tau, V if tau == 11 else S)
        pump(12)
        qx(4)
        qx(5)
        for e, G in ((1, 0), (1, 1)):
            for c in range(4):
                sup(e, G, c)
            for c in range(4):
                cs(e, G, c, V if c == 3 else S)
            if (e, G) == (1, 0):
                rw(2, 0, 128)
                rw(2, 1, 128)
            if (e, G) == (1, 1):
                qs(1, 0)
                qw(2, 0)
                qw(2, 1)
        turn_rows(0)
        vt(0)
        for kind in ("r", "g"):
            for o in range(2):
                ca(kind, 0, o, S)
        for c in range(4):
            sup(0, 2, c)
        qs(1, 1)
        qa("r", 0)
        for c in range(4):
            cs(0, 2, c, V if c == 3 else S)
        qa("g", 0)
        for c in range(4):
            sup(1, 2, c)
        cz(0, 0, S)
        cz(0, 1, V)
        qs(0, 2)
        for c in range(4):
            cs(1, 2, c, V if c == 3 else S)
        qa("z", 0)
        turn_rows(1)
        pump(18)
        qs(1, 2)
        prepare(1)
        for u in range(6):
            for q in range(2):
                out_tile(u, q, 256 if (u, q) == (5, 1) else 512)
            if u in (0, 2):
                turn_rows(u + 2)
                turn_rows(u + 3)
                prepare(u + 2)
                prepare(u + 3)
